import numpy as np
import ml_dtypes

BF16 = ml_dtypes.bfloat16


def bf(x):
    return np.asarray(x, np.float32).astype(BF16)


def f32(x):
    return np.asarray(x, np.float32)


def f64(x):
    return np.asarray(x).astype(np.float64)


def striped(idx):
    return np.tile(idx.reshape(-1, 16).T, (8, 1))


D, S, Q, R, H, N = 128, 512, 256, 8, 256, 2048
LEAKY = 0.01
ATT_STD = 1.414 * np.sqrt(2.0 / (1 + 2 * D))


def setup_inputs():
    table = bf(np.random.standard_normal((D, S)))
    w_ref = bf(np.tile(ATT_STD * np.random.standard_normal((D, 1)), (1, D)))
    w_nei = bf(np.tile(ATT_STD * np.random.standard_normal((D, 1)), (1, D)))
    idx = np.concatenate([np.random.permutation(S)[:H] for _ in range(R)])
    return {"table": table, "w_ref": w_ref, "w_nei": w_nei, "offs": striped(idx)}


def reference(table, w_ref, w_nei, offs):
    idx = offs[:16].T.reshape(-1)
    t = f64(table)
    nei = t[:, idx]
    s = (f64(w_nei).T @ nei).reshape(D, R, Q) + (f64(w_ref).T @ t[:, :Q])[:, None, :]
    l = np.where(s >= 0, s, LEAKY * s)
    e = np.exp(l)
    a = e / e.sum(axis=1, keepdims=True)
    o = (a * nei.reshape(D, R, Q)).sum(axis=1)
    return np.where(o > 0, o, np.exp(np.minimum(o, 0.0)) - 1.0)

@@ -1,0 +1,90 @@
+import concourse.mybir as mybir
+from concourse.masks import make_identity
+
+BF16 = mybir.dt.bfloat16
+F32 = mybir.dt.float32
+U16 = mybir.dt.uint16
+ALU = mybir.AluOpType
+ACT = mybir.ActivationFunctionType
+X = mybir.AxisListType.X
+
+P = 128
+NODES = 512
+Q = 256
+R = 8
+N = R * Q
+BANK = 512
+RUNS = BANK // Q
+BANKS = N // BANK
+SLOPE = 0.01
+
+FLOPS = 2 * P * P * (N + Q)
+
+
+def tile_feat_encoder_kernel(tc, table, w_ref, w_nei, offs, out):
+    nc = tc.nc
+    with (
+        tc.tile_pool(name="held", bufs=1) as held,
+        tc.psum_pool(name="psum", bufs=1) as psum,
+    ):
+        store = held.tile([P, NODES], BF16, name="store")
+        nc.scalar.dma_start(store[:], table)
+        ref_w = held.tile([P, P], BF16, name="ref_w")
+        nc.sync.dma_start(ref_w[:], w_ref)
+        offsets = held.tile([P, N // 16], U16, name="offsets")
+        nc.sync.dma_start(offsets[:], offs)
+        nei_w = held.tile([P, P], BF16, name="nei_w")
+        nc.scalar.dma_start(nei_w[:], w_nei)
+        ident = held.tile([P, P], BF16, name="ident")
+        make_identity(nc, ident[:])
+
+        score = [psum.tile([P, BANK], F32, name=f"score{b}") for b in range(BANKS)]
+        own = store[:, 0:Q].unsqueeze(1).to_broadcast([P, RUNS, Q])
+        for b in range(BANKS):
+            nc.tensor.matmul(score[b][:].rearrange("p (t q) -> p t q", q=Q), ref_w[:], own, start=True, stop=False)
+        for r in range(R):
+            b, t = divmod(r, RUNS)
+            piece = offsets[:, r * (Q // 16) : (r + 1) * (Q // 16)]
+            nc.tensor.matmul(
+                score[b][:, t * Q : (t + 1) * Q], nei_w[:], store[:].indirect(piece), start=False, stop=(t == RUNS - 1)
+            )
+
+        feat = [psum.tile([P, BANK], F32, name=f"feat{b}") for b in range(BANKS)]
+        for b in range(BANKS):
+            piece = offsets[:, b * (BANK // 16) : (b + 1) * (BANK // 16)]
+            nc.tensor.matmul(feat[b][:], ident[:], store[:].indirect(piece), start=True, stop=True)
+
+        raw = held.tile([P, N], F32, name="raw")
+        leaky = held.tile([P, N], F32, name="leaky")
+        for b in range(BANKS):
+            cols = slice(b * BANK, (b + 1) * BANK)
+            nc.scalar.copy(raw[:, cols], score[b][:])
+            nc.vector.scalar_tensor_tensor(leaky[:, cols], score[b][:], SLOPE, raw[:, cols], ALU.mult, ALU.max)
+
+        top = held.tile([P, Q], F32, name="top")
+        nc.vector.tensor_reduce(top[:], leaky[:].rearrange("p (r q) -> p q r", q=Q), axis=X, op=ALU.max)
+        by_run = leaky[:].rearrange("p (r q) -> p r q", q=Q)
+        nc.vector.tensor_tensor(by_run, by_run, top[:].unsqueeze(1).to_broadcast([P, R, Q]), ALU.subtract)
+        weight = held.tile([P, N], F32, name="weight")
+        nc.scalar.activation(weight[:], leaky[:], ACT.Exp)
+        den = held.tile([P, Q], F32, name="den")
+        nc.vector.tensor_reduce(den[:], weight[:].rearrange("p (r q) -> p q r", q=Q), axis=X, op=ALU.add)
+
+        prod = held.tile([P, N], F32, name="prod")
+        for b in range(BANKS):
+            cols = slice(b * BANK, (b + 1) * BANK)
+            nc.vector.tensor_tensor(prod[:, cols], weight[:, cols], feat[b][:], ALU.mult)
+        num = held.tile([P, Q], F32, name="num")
+        nc.vector.tensor_reduce(num[:], prod[:].rearrange("p (r q) -> p q r", q=Q), axis=X, op=ALU.add)
+        rden = held.tile([P, Q], F32, name="rden")
+        nc.vector.reciprocal(rden[:], den[:])
+        mean = held.tile([P, Q], F32, name="mean")
+        nc.vector.tensor_tensor(mean[:], num[:], rden[:], ALU.mult)
+
+        neg = held.tile([P, Q], F32, name="neg")
+        nc.vector.tensor_scalar_min(neg[:], mean[:], 0.0)
+        grown = held.tile([P, Q], F32, name="grown")
+        nc.scalar.activation(grown[:], neg[:], ACT.Exp)
+        result = held.tile([P, Q], F32, name="result")
+        nc.vector.scalar_tensor_tensor(result[:], grown[:], -1.0, mean[:], ALU.add, ALU.max)
+        nc.sync.dma_start(out, result[:])

@@ -6,7 +6,6 @@ F32 = mybir.dt.float32
 U16 = mybir.dt.uint16
 ALU = mybir.AluOpType
 ACT = mybir.ActivationFunctionType
-X = mybir.AxisListType.X
 
 P = 128
 NODES = 512
@@ -19,6 +18,13 @@ BANKS = N // BANK
 SLOPE = 0.01
 
 FLOPS = 2 * P * P * (N + Q)
+
+
+def fold_runs(nc, op, narrow, wide, banks):
+    nc.vector.tensor_tensor(wide[:], banks[0][:], banks[1][:], op)
+    for bank in banks[2:]:
+        nc.vector.tensor_tensor(wide[:], wide[:], bank[:], op)
+    nc.vector.tensor_tensor(narrow[:], wide[:, 0:Q], wide[:, Q:BANK], op)
 
 
 def tile_feat_encoder_kernel(tc, table, w_ref, w_nei, offs, out):
@@ -54,28 +60,29 @@ def tile_feat_encoder_kernel(tc, table, w_ref, w_nei, offs, out):
             piece = offsets[:, b * (BANK // 16) : (b + 1) * (BANK // 16)]
             nc.tensor.matmul(feat[b][:], ident[:], store[:].indirect(piece), start=True, stop=True)
 
-        raw = held.tile([P, N], F32, name="raw")
-        leaky = held.tile([P, N], F32, name="leaky")
+        raw = [held.tile([P, BANK], F32, name=f"raw{b}") for b in range(BANKS)]
+        leaky = [held.tile([P, BANK], F32, name=f"leaky{b}") for b in range(BANKS)]
         for b in range(BANKS):
-            cols = slice(b * BANK, (b + 1) * BANK)
-            nc.scalar.copy(raw[:, cols], score[b][:])
-            nc.vector.scalar_tensor_tensor(leaky[:, cols], score[b][:], SLOPE, raw[:, cols], ALU.mult, ALU.max)
+            nc.scalar.copy(raw[b][:], score[b][:])
+            nc.vector.scalar_tensor_tensor(leaky[b][:], score[b][:], SLOPE, raw[b][:], ALU.mult, ALU.max)
 
         top = held.tile([P, Q], F32, name="top")
-        nc.vector.tensor_reduce(top[:], leaky[:].rearrange("p (r q) -> p q r", q=Q), axis=X, op=ALU.max)
-        by_run = leaky[:].rearrange("p (r q) -> p r q", q=Q)
-        nc.vector.tensor_tensor(by_run, by_run, top[:].unsqueeze(1).to_broadcast([P, R, Q]), ALU.subtract)
-        weight = held.tile([P, N], F32, name="weight")
-        nc.scalar.activation(weight[:], leaky[:], ACT.Exp)
-        den = held.tile([P, Q], F32, name="den")
-        nc.vector.tensor_reduce(den[:], weight[:].rearrange("p (r q) -> p q r", q=Q), axis=X, op=ALU.add)
-
-        prod = held.tile([P, N], F32, name="prod")
+        top_wide = held.tile([P, BANK], F32, name="top_wide")
+        fold_runs(nc, ALU.max, top, top_wide, leaky)
+        top_runs = top[:].unsqueeze(1).to_broadcast([P, RUNS, Q])
+        weight = [held.tile([P, BANK], F32, name=f"weight{b}") for b in range(BANKS)]
+        prod = [held.tile([P, BANK], F32, name=f"prod{b}") for b in range(BANKS)]
         for b in range(BANKS):
-            cols = slice(b * BANK, (b + 1) * BANK)
-            nc.vector.tensor_tensor(prod[:, cols], weight[:, cols], feat[b][:], ALU.mult)
+            by_run = leaky[b][:].rearrange("p (t q) -> p t q", q=Q)
+            nc.vector.tensor_tensor(by_run, by_run, top_runs, ALU.subtract)
+            nc.scalar.activation(weight[b][:], leaky[b][:], ACT.Exp)
+            nc.vector.tensor_tensor(prod[b][:], weight[b][:], feat[b][:], ALU.mult)
+        den = held.tile([P, Q], F32, name="den")
+        den_wide = held.tile([P, BANK], F32, name="den_wide")
+        fold_runs(nc, ALU.add, den, den_wide, weight)
         num = held.tile([P, Q], F32, name="num")
-        nc.vector.tensor_reduce(num[:], prod[:].rearrange("p (r q) -> p q r", q=Q), axis=X, op=ALU.add)
+        num_wide = held.tile([P, BANK], F32, name="num_wide")
+        fold_runs(nc, ALU.add, num, num_wide, prod)
         rden = held.tile([P, Q], F32, name="rden")
         nc.vector.reciprocal(rden[:], den[:])
         mean = held.tile([P, Q], F32, name="mean")

@@ -31,7 +31,7 @@ def tile_feat_encoder_kernel(tc, table, w_ref, w_nei, offs, out):
     nc = tc.nc
     with (
         tc.tile_pool(name="held", bufs=1) as held,
-        tc.psum_pool(name="psum", bufs=1) as psum,
+        tc.psum_pool(name="psum", bufs=BANKS) as psum,
     ):
         store = held.tile([P, NODES], BF16, name="store")
         nc.scalar.dma_start(store[:], table)
@@ -43,8 +43,10 @@ def tile_feat_encoder_kernel(tc, table, w_ref, w_nei, offs, out):
         nc.scalar.dma_start(nei_w[:], w_nei)
         ident = held.tile([P, P], BF16, name="ident")
         make_identity(nc, ident[:])
+        ident_f = held.tile([P, P], F32, name="ident_f")
+        make_identity(nc, ident_f[:])
 
-        score = [psum.tile([P, BANK], F32, name=f"score{b}") for b in range(BANKS)]
+        score = [psum.tile([P, BANK], F32, name=f"score{b}", tag="score") for b in range(BANKS)]
         own = store[:, 0:Q].unsqueeze(1).to_broadcast([P, RUNS, Q])
         for b in range(BANKS):
             nc.tensor.matmul(score[b][:].rearrange("p (t q) -> p t q", q=Q), ref_w[:], own, start=True, stop=False)
@@ -55,7 +57,7 @@ def tile_feat_encoder_kernel(tc, table, w_ref, w_nei, offs, out):
                 score[b][:, t * Q : (t + 1) * Q], nei_w[:], store[:].indirect(piece), start=False, stop=(t == RUNS - 1)
             )
 
-        feat = [psum.tile([P, BANK], F32, name=f"feat{b}") for b in range(BANKS)]
+        feat = [psum.tile([P, BANK], F32, name=f"feat{b}", tag="feat") for b in range(BANKS)]
         for b in range(BANKS):
             piece = offsets[:, b * (BANK // 16) : (b + 1) * (BANK // 16)]
             nc.tensor.matmul(feat[b][:], ident[:], store[:].indirect(piece), start=True, stop=True)
@@ -77,9 +79,10 @@ def tile_feat_encoder_kernel(tc, table, w_ref, w_nei, offs, out):
             nc.vector.tensor_tensor(by_run, by_run, top_runs, ALU.subtract)
             nc.scalar.activation(weight[b][:], leaky[b][:], ACT.Exp)
             nc.vector.tensor_tensor(prod[b][:], weight[b][:], feat[b][:], ALU.mult)
-        den = held.tile([P, Q], F32, name="den")
-        den_wide = held.tile([P, BANK], F32, name="den_wide")
-        fold_runs(nc, ALU.add, den, den_wide, weight)
+        den = psum.tile([P, Q], F32, name="den", tag="score")
+        for r in range(R):
+            b, t = divmod(r, RUNS)
+            nc.tensor.matmul(den[:], ident_f[:], weight[b][:, t * Q : (t + 1) * Q], start=(r == 0), stop=(r == R - 1))
         num = held.tile([P, Q], F32, name="num")
         num_wide = held.tile([P, BANK], F32, name="num_wide")
         fold_runs(nc, ALU.add, num, num_wide, prod)

@@ -16,15 +16,9 @@ BANK = 512
 RUNS = BANK // Q
 BANKS = N // BANK
 SLOPE = 0.01
+WARM_UPS = 4
 
 FLOPS = 2 * P * P * (N + Q)
-
-
-def fold_runs(nc, op, narrow, wide, banks):
-    nc.vector.tensor_tensor(wide[:], banks[0][:], banks[1][:], op)
-    for bank in banks[2:]:
-        nc.vector.tensor_tensor(wide[:], wide[:], bank[:], op)
-    nc.vector.tensor_tensor(narrow[:], wide[:, 0:Q], wide[:, Q:BANK], op)
 
 
 def tile_feat_encoder_kernel(tc, table, w_ref, w_nei, offs, out):
@@ -46,6 +40,12 @@ def tile_feat_encoder_kernel(tc, table, w_ref, w_nei, offs, out):
         ident_f = held.tile([P, P], F32, name="ident_f")
         make_identity(nc, ident_f[:])
 
+        zeros = held.tile([P, BANK], BF16, name="zeros")
+        nc.vector.memset(zeros[:], 0.0)
+        idle = psum.tile([P, BANK], F32, name="idle", tag="feat")
+        for i in range(WARM_UPS):
+            nc.tensor.matmul(idle[:], zeros[:, 0:P], zeros[:], start=True, stop=True)
+
         score = [psum.tile([P, BANK], F32, name=f"score{b}", tag="score") for b in range(BANKS)]
         own = store[:, 0:Q].unsqueeze(1).to_broadcast([P, RUNS, Q])
         for b in range(BANKS):
@@ -64,37 +64,44 @@ def tile_feat_encoder_kernel(tc, table, w_ref, w_nei, offs, out):
 
         raw = [held.tile([P, BANK], F32, name=f"raw{b}") for b in range(BANKS)]
         leaky = [held.tile([P, BANK], F32, name=f"leaky{b}") for b in range(BANKS)]
+        top_wide = held.tile([P, BANK], F32, name="top_wide")
         for b in range(BANKS):
             nc.scalar.copy(raw[b][:], score[b][:])
             nc.vector.scalar_tensor_tensor(leaky[b][:], score[b][:], SLOPE, raw[b][:], ALU.mult, ALU.max)
-
+            if b > 0:
+                nc.vector.tensor_tensor(top_wide[:], leaky[0][:] if b == 1 else top_wide[:], leaky[b][:], ALU.max)
         top = held.tile([P, Q], F32, name="top")
-        top_wide = held.tile([P, BANK], F32, name="top_wide")
-        fold_runs(nc, ALU.max, top, top_wide, leaky)
+        nc.vector.tensor_tensor(top[:], top_wide[:, 0:Q], top_wide[:, Q:BANK], ALU.max)
+
         top_runs = top[:].unsqueeze(1).to_broadcast([P, RUNS, Q])
         weight = [held.tile([P, BANK], F32, name=f"weight{b}") for b in range(BANKS)]
-        prod = [held.tile([P, BANK], F32, name=f"prod{b}") for b in range(BANKS)]
         for b in range(BANKS):
             by_run = leaky[b][:].rearrange("p (t q) -> p t q", q=Q)
             nc.vector.tensor_tensor(by_run, by_run, top_runs, ALU.subtract)
             nc.scalar.activation(weight[b][:], leaky[b][:], ACT.Exp)
-            nc.vector.tensor_tensor(prod[b][:], weight[b][:], feat[b][:], ALU.mult)
+
         den = psum.tile([P, Q], F32, name="den", tag="score")
         for r in range(R):
             b, t = divmod(r, RUNS)
             nc.tensor.matmul(den[:], ident_f[:], weight[b][:, t * Q : (t + 1) * Q], start=(r == 0), stop=(r == R - 1))
-        num = held.tile([P, Q], F32, name="num")
-        num_wide = held.tile([P, BANK], F32, name="num_wide")
-        fold_runs(nc, ALU.add, num, num_wide, prod)
         rden = held.tile([P, Q], F32, name="rden")
         nc.vector.reciprocal(rden[:], den[:])
-        mean = held.tile([P, Q], F32, name="mean")
-        nc.vector.tensor_tensor(mean[:], num[:], rden[:], ALU.mult)
+
+        prod = [held.tile([P, BANK], F32, name=f"prod{b}") for b in range(BANKS)]
+        num_wide = held.tile([P, BANK], F32, name="num_wide")
+        for b in range(BANKS):
+            nc.vector.tensor_tensor(prod[b][:], weight[b][:], feat[b][:], ALU.mult)
+            if b > 0:
+                nc.vector.tensor_tensor(num_wide[:], prod[0][:] if b == 1 else num_wide[:], prod[b][:], ALU.add)
+        num = held.tile([P, Q], F32, name="num")
+        nc.vector.tensor_tensor(num[:], num_wide[:, 0:Q], num_wide[:, Q:BANK], ALU.add)
 
         neg = held.tile([P, Q], F32, name="neg")
-        nc.vector.tensor_scalar_min(neg[:], mean[:], 0.0)
+        nc.vector.scalar_tensor_tensor(neg[:], num[:], 0.0, rden[:], ALU.min, ALU.mult)
         grown = held.tile([P, Q], F32, name="grown")
         nc.scalar.activation(grown[:], neg[:], ACT.Exp)
+        mean = held.tile([P, Q], F32, name="mean")
+        nc.vector.tensor_tensor(mean[:], num[:], rden[:], ALU.mult)
         result = held.tile([P, Q], F32, name="result")
         nc.vector.scalar_tensor_tensor(result[:], grown[:], -1.0, mean[:], ALU.add, ALU.max)
         nc.sync.dma_start(out, result[:])

@@ -6,6 +6,7 @@ F32 = mybir.dt.float32
 U16 = mybir.dt.uint16
 ALU = mybir.AluOpType
 ACT = mybir.ActivationFunctionType
+X = mybir.AxisListType.X
 
 P = 128
 NODES = 512
@@ -16,7 +17,10 @@ BANK = 512
 RUNS = BANK // Q
 BANKS = N // BANK
 SLOPE = 0.01
-WARM_UPS = 4
+SIDE = 32
+PACKED = N // SIDE
+PACKED_RUN = Q // SIDE
+PACKED_BANK = BANK // SIDE
 
 FLOPS = 2 * P * P * (N + Q)
 
@@ -37,14 +41,6 @@ def tile_feat_encoder_kernel(tc, table, w_ref, w_nei, offs, out):
         nc.scalar.dma_start(nei_w[:], w_nei)
         ident = held.tile([P, P], BF16, name="ident")
         make_identity(nc, ident[:])
-        ident_f = held.tile([P, P], F32, name="ident_f")
-        make_identity(nc, ident_f[:])
-
-        zeros = held.tile([P, BANK], BF16, name="zeros")
-        nc.vector.memset(zeros[:], 0.0)
-        idle = psum.tile([P, BANK], F32, name="idle", tag="feat")
-        for i in range(WARM_UPS):
-            nc.tensor.matmul(idle[:], zeros[:, 0:P], zeros[:], start=True, stop=True)
 
         score = [psum.tile([P, BANK], F32, name=f"score{b}", tag="score") for b in range(BANKS)]
         own = store[:, 0:Q].unsqueeze(1).to_broadcast([P, RUNS, Q])
@@ -62,46 +58,48 @@ def tile_feat_encoder_kernel(tc, table, w_ref, w_nei, offs, out):
             piece = offsets[:, b * (BANK // 16) : (b + 1) * (BANK // 16)]
             nc.tensor.matmul(feat[b][:], ident[:], store[:].indirect(piece), start=True, stop=True)
 
-        raw = [held.tile([P, BANK], F32, name=f"raw{b}") for b in range(BANKS)]
-        leaky = [held.tile([P, BANK], F32, name=f"leaky{b}") for b in range(BANKS)]
-        top_wide = held.tile([P, BANK], F32, name="top_wide")
+        flipped = held.tile([P, N], F32, name="flipped", align_bytes=64)
         for b in range(BANKS):
-            nc.scalar.copy(raw[b][:], score[b][:])
-            nc.vector.scalar_tensor_tensor(leaky[b][:], score[b][:], SLOPE, raw[b][:], ALU.mult, ALU.max)
-            if b > 0:
-                nc.vector.tensor_tensor(top_wide[:], leaky[0][:] if b == 1 else top_wide[:], leaky[b][:], ALU.max)
-        top = held.tile([P, Q], F32, name="top")
-        nc.vector.tensor_tensor(top[:], top_wide[:, 0:Q], top_wide[:, Q:BANK], ALU.max)
+            nc.vector.transpose(flipped[:, b * BANK : (b + 1) * BANK], score[b][:])
+        packed = flipped[:].rearrange("p (j w) -> p j w", w=SIDE)[:, :, 0]
 
-        top_runs = top[:].unsqueeze(1).to_broadcast([P, RUNS, Q])
-        weight = [held.tile([P, BANK], F32, name=f"weight{b}") for b in range(BANKS)]
-        for b in range(BANKS):
-            by_run = leaky[b][:].rearrange("p (t q) -> p t q", q=Q)
-            nc.vector.tensor_tensor(by_run, by_run, top_runs, ALU.subtract)
-            nc.scalar.activation(weight[b][:], leaky[b][:], ACT.Exp)
-
-        den = psum.tile([P, Q], F32, name="den", tag="score")
-        for r in range(R):
-            b, t = divmod(r, RUNS)
-            nc.tensor.matmul(den[:], ident_f[:], weight[b][:, t * Q : (t + 1) * Q], start=(r == 0), stop=(r == R - 1))
-        rden = held.tile([P, Q], F32, name="rden")
+        leaky = held.tile([P, PACKED], F32, name="leaky")
+        nc.vector.scalar_tensor_tensor(leaky[:], packed, SLOPE, packed, ALU.mult, ALU.max)
+        top = held.tile([P, PACKED_RUN], F32, name="top")
+        nc.vector.tensor_reduce(top[:], leaky[:].rearrange("p (r g) -> p g r", g=PACKED_RUN), axis=X, op=ALU.max)
+        leaky_runs = leaky[:].rearrange("p (r g) -> p r g", g=PACKED_RUN)
+        nc.vector.tensor_tensor(
+            leaky_runs, leaky_runs, top[:].unsqueeze(1).to_broadcast([P, R, PACKED_RUN]), ALU.subtract
+        )
+        weight = held.tile([P, PACKED], F32, name="weight")
+        nc.scalar.activation(weight[:], leaky[:], ACT.Exp)
+        den = held.tile([P, PACKED_RUN], F32, name="den")
+        nc.vector.tensor_reduce(den[:], weight[:].rearrange("p (r g) -> p g r", g=PACKED_RUN), axis=X, op=ALU.add)
+        rden = held.tile([P, PACKED_RUN], F32, name="rden")
         nc.vector.reciprocal(rden[:], den[:])
+        weight_runs = weight[:].rearrange("p (r g) -> p r g", g=PACKED_RUN)
+        nc.vector.tensor_tensor(
+            weight_runs, weight_runs, rden[:].unsqueeze(1).to_broadcast([P, R, PACKED_RUN]), ALU.mult
+        )
 
         prod = [held.tile([P, BANK], F32, name=f"prod{b}") for b in range(BANKS)]
-        num_wide = held.tile([P, BANK], F32, name="num_wide")
+        sum_wide = held.tile([P, BANK], F32, name="sum_wide")
         for b in range(BANKS):
-            nc.vector.tensor_tensor(prod[b][:], weight[b][:], feat[b][:], ALU.mult)
+            some = weight[:, b * PACKED_BANK : (b + 1) * PACKED_BANK].unsqueeze(2).to_broadcast([P, PACKED_BANK, SIDE])
+            spread = held.tile([P, BANK], F32, name=f"spread{b}", align_bytes=64)
+            nc.scalar.copy(spread[:].rearrange("p (j w) -> p j w", w=SIDE), some)
+            row = held.tile([P, BANK], F32, name=f"row{b}", align_bytes=64)
+            nc.vector.transpose(row[:], spread[:])
+            nc.vector.tensor_tensor(prod[b][:], row[:], feat[b][:], ALU.mult)
             if b > 0:
-                nc.vector.tensor_tensor(num_wide[:], prod[0][:] if b == 1 else num_wide[:], prod[b][:], ALU.add)
-        num = held.tile([P, Q], F32, name="num")
-        nc.vector.tensor_tensor(num[:], num_wide[:, 0:Q], num_wide[:, Q:BANK], ALU.add)
+                nc.vector.tensor_tensor(sum_wide[:], prod[0][:] if b == 1 else sum_wide[:], prod[b][:], ALU.add)
+        mean = held.tile([P, Q], F32, name="mean")
+        nc.vector.tensor_tensor(mean[:], sum_wide[:, 0:Q], sum_wide[:, Q:BANK], ALU.add)
 
         neg = held.tile([P, Q], F32, name="neg")
-        nc.vector.scalar_tensor_tensor(neg[:], num[:], 0.0, rden[:], ALU.min, ALU.mult)
+        nc.vector.tensor_scalar_min(neg[:], mean[:], 0.0)
         grown = held.tile([P, Q], F32, name="grown")
         nc.scalar.activation(grown[:], neg[:], ACT.Exp)
-        mean = held.tile([P, Q], F32, name="mean")
-        nc.vector.tensor_tensor(mean[:], num[:], rden[:], ALU.mult)
         result = held.tile([P, Q], F32, name="result")
         nc.vector.scalar_tensor_tensor(result[:], grown[:], -1.0, mean[:], ALU.add, ALU.max)
         nc.sync.dma_start(out, result[:])

@@ -17,6 +17,7 @@ BANK = 512
 RUNS = BANK // Q
 BANKS = N // BANK
 SLOPE = 0.01
+WARM_UPS = 2
 SIDE = 32
 PACKED = N // SIDE
 PACKED_RUN = Q // SIDE
@@ -42,29 +43,41 @@ def tile_feat_encoder_kernel(tc, table, w_ref, w_nei, offs, out):
         ident = held.tile([P, P], BF16, name="ident")
         make_identity(nc, ident[:])
 
-        score = [psum.tile([P, BANK], F32, name=f"score{b}", tag="score") for b in range(BANKS)]
-        own = store[:, 0:Q].unsqueeze(1).to_broadcast([P, RUNS, Q])
-        for b in range(BANKS):
-            nc.tensor.matmul(score[b][:].rearrange("p (t q) -> p t q", q=Q), ref_w[:], own, start=True, stop=False)
-        for r in range(R):
-            b, t = divmod(r, RUNS)
-            piece = offsets[:, r * (Q // 16) : (r + 1) * (Q // 16)]
-            nc.tensor.matmul(
-                score[b][:, t * Q : (t + 1) * Q], nei_w[:], store[:].indirect(piece), start=False, stop=(t == RUNS - 1)
-            )
+        zeros = held.tile([P, BANK], BF16, name="zeros")
+        nc.vector.memset(zeros[:], 0.0)
+        idle = psum.tile([P, BANK], F32, name="idle", tag="score")
+        for i in range(WARM_UPS):
+            nc.tensor.matmul(idle[:], zeros[:, 0:P], zeros[:], start=True, stop=True)
 
+        own = psum.tile([P, Q], F32, name="own", tag="feat")
+        nc.tensor.matmul(own[:], ref_w[:], store[:, 0:Q], start=True, stop=True)
+
+        pieces = [offsets[:, b * (BANK // 16) : (b + 1) * (BANK // 16)] for b in range(BANKS)]
+        score = [psum.tile([P, BANK], F32, name=f"score{b}", tag="score") for b in range(BANKS)]
+        for b in range(BANKS):
+            nc.tensor.matmul(score[b][:], nei_w[:], store[:].indirect(pieces[b]), start=True, stop=True)
         feat = [psum.tile([P, BANK], F32, name=f"feat{b}", tag="feat") for b in range(BANKS)]
         for b in range(BANKS):
-            piece = offsets[:, b * (BANK // 16) : (b + 1) * (BANK // 16)]
-            nc.tensor.matmul(feat[b][:], ident[:], store[:].indirect(piece), start=True, stop=True)
+            nc.tensor.matmul(feat[b][:], ident[:], store[:].indirect(pieces[b]), start=True, stop=True)
 
-        flipped = held.tile([P, N], F32, name="flipped", align_bytes=64)
+        own_flipped = held.tile([P, Q], F32, name="own_flipped", align_bytes=64)
+        for h in range(Q // P):
+            nc.vector.transpose(own_flipped[:, h * P : (h + 1) * P], own[:, h * P : (h + 1) * P])
+        own_packed = own_flipped[:].rearrange("p (g w) -> p g w", w=SIDE)[:, :, 0]
+        score_flipped = held.tile([P, N], F32, name="score_flipped", align_bytes=64)
         for b in range(BANKS):
-            nc.vector.transpose(flipped[:, b * BANK : (b + 1) * BANK], score[b][:])
-        packed = flipped[:].rearrange("p (j w) -> p j w", w=SIDE)[:, :, 0]
+            nc.vector.transpose(score_flipped[:, b * BANK : (b + 1) * BANK], score[b][:])
+        score_packed = score_flipped[:].rearrange("p (r g w) -> p r g w", g=PACKED_RUN, w=SIDE)[:, :, :, 0]
 
+        total = held.tile([P, PACKED], F32, name="total")
+        nc.vector.tensor_tensor(
+            total[:].rearrange("p (r g) -> p r g", g=PACKED_RUN),
+            score_packed,
+            own_packed.unsqueeze(1).to_broadcast([P, R, PACKED_RUN]),
+            ALU.add,
+        )
         leaky = held.tile([P, PACKED], F32, name="leaky")
-        nc.vector.scalar_tensor_tensor(leaky[:], packed, SLOPE, packed, ALU.mult, ALU.max)
+        nc.vector.scalar_tensor_tensor(leaky[:], total[:], SLOPE, total[:], ALU.mult, ALU.max)
         top = held.tile([P, PACKED_RUN], F32, name="top")
         nc.vector.tensor_reduce(top[:], leaky[:].rearrange("p (r g) -> p g r", g=PACKED_RUN), axis=X, op=ALU.max)
         leaky_runs = leaky[:].rearrange("p (r g) -> p r g", g=PACKED_RUN)
@@ -77,29 +90,37 @@ def tile_feat_encoder_kernel(tc, table, w_ref, w_nei, offs, out):
         nc.vector.tensor_reduce(den[:], weight[:].rearrange("p (r g) -> p g r", g=PACKED_RUN), axis=X, op=ALU.add)
         rden = held.tile([P, PACKED_RUN], F32, name="rden")
         nc.vector.reciprocal(rden[:], den[:])
-        weight_runs = weight[:].rearrange("p (r g) -> p r g", g=PACKED_RUN)
-        nc.vector.tensor_tensor(
-            weight_runs, weight_runs, rden[:].unsqueeze(1).to_broadcast([P, R, PACKED_RUN]), ALU.mult
-        )
 
+        num_wide = held.tile([P, BANK], F32, name="num_wide")
+        feat_flipped = [held.tile([P, BANK], F32, name=f"feat_flipped{b}", align_bytes=64) for b in range(BANKS)]
         prod = [held.tile([P, BANK], F32, name=f"prod{b}") for b in range(BANKS)]
-        sum_wide = held.tile([P, BANK], F32, name="sum_wide")
         for b in range(BANKS):
-            some = weight[:, b * PACKED_BANK : (b + 1) * PACKED_BANK].unsqueeze(2).to_broadcast([P, PACKED_BANK, SIDE])
-            spread = held.tile([P, BANK], F32, name=f"spread{b}", align_bytes=64)
-            nc.scalar.copy(spread[:].rearrange("p (j w) -> p j w", w=SIDE), some)
-            row = held.tile([P, BANK], F32, name=f"row{b}", align_bytes=64)
-            nc.vector.transpose(row[:], spread[:])
-            nc.vector.tensor_tensor(prod[b][:], row[:], feat[b][:], ALU.mult)
+            nc.vector.transpose(feat_flipped[b][:], feat[b][:])
+        for b in range(BANKS):
+            nc.vector.tensor_tensor(
+                prod[b][:].rearrange("p (j w) -> p j w", w=SIDE),
+                feat_flipped[b][:].rearrange("p (j w) -> p j w", w=SIDE),
+                weight[:, b * PACKED_BANK : (b + 1) * PACKED_BANK].unsqueeze(2).to_broadcast([P, PACKED_BANK, SIDE]),
+                ALU.mult,
+            )
             if b > 0:
-                nc.vector.tensor_tensor(sum_wide[:], prod[0][:] if b == 1 else sum_wide[:], prod[b][:], ALU.add)
-        mean = held.tile([P, Q], F32, name="mean")
-        nc.vector.tensor_tensor(mean[:], sum_wide[:, 0:Q], sum_wide[:, Q:BANK], ALU.add)
+                nc.vector.tensor_tensor(num_wide[:], prod[0][:] if b == 1 else num_wide[:], prod[b][:], ALU.add)
+        num = held.tile([P, Q], F32, name="num")
+        nc.vector.tensor_tensor(num[:], num_wide[:, 0:Q], num_wide[:, Q:BANK], ALU.add)
 
+        num_blocks = num[:].rearrange("p (g w) -> p g w", w=SIDE)
+        rden_blocks = rden[:].unsqueeze(2).to_broadcast([P, PACKED_RUN, SIDE])
         neg = held.tile([P, Q], F32, name="neg")
-        nc.vector.tensor_scalar_min(neg[:], mean[:], 0.0)
+        nc.vector.scalar_tensor_tensor(
+            neg[:].rearrange("p (g w) -> p g w", w=SIDE), num_blocks, 0.0, rden_blocks, ALU.min, ALU.mult
+        )
         grown = held.tile([P, Q], F32, name="grown")
         nc.scalar.activation(grown[:], neg[:], ACT.Exp)
-        result = held.tile([P, Q], F32, name="result")
-        nc.vector.scalar_tensor_tensor(result[:], grown[:], -1.0, mean[:], ALU.add, ALU.max)
+        mean = held.tile([P, Q], F32, name="mean")
+        nc.vector.tensor_tensor(mean[:].rearrange("p (g w) -> p g w", w=SIDE), num_blocks, rden_blocks, ALU.mult)
+        result_flipped = held.tile([P, Q], F32, name="result_flipped", align_bytes=64)
+        nc.vector.scalar_tensor_tensor(result_flipped[:], grown[:], -1.0, mean[:], ALU.add, ALU.max)
+
+        result = held.tile([P, Q], F32, name="result", align_bytes=64)
+        nc.vector.transpose(result[:], result_flipped[:])
         nc.sync.dma_start(out, result[:])

@@ -17,7 +17,6 @@ BANK = 512
 RUNS = BANK // Q
 BANKS = N // BANK
 SLOPE = 0.01
-WARM_UPS = 2
 SIDE = 32
 PACKED = N // SIDE
 PACKED_RUN = Q // SIDE
@@ -42,12 +41,6 @@ def tile_feat_encoder_kernel(tc, table, w_ref, w_nei, offs, out):
         nc.scalar.dma_start(nei_w[:], w_nei)
         ident = held.tile([P, P], BF16, name="ident")
         make_identity(nc, ident[:])
-
-        zeros = held.tile([P, BANK], BF16, name="zeros")
-        nc.vector.memset(zeros[:], 0.0)
-        idle = psum.tile([P, BANK], F32, name="idle", tag="score")
-        for i in range(WARM_UPS):
-            nc.tensor.matmul(idle[:], zeros[:, 0:P], zeros[:], start=True, stop=True)
 
         own = psum.tile([P, Q], F32, name="own", tag="feat")
         nc.tensor.matmul(own[:], ref_w[:], store[:, 0:Q], start=True, stop=True)

@@ -21,6 +21,7 @@ SIDE = 32
 PACKED = N // SIDE
 PACKED_RUN = Q // SIDE
 PACKED_BANK = BANK // SIDE
+COPIES = SIDE // R
 
 FLOPS = 2 * P * P * (N + Q)
 
@@ -42,35 +43,39 @@ def tile_feat_encoder_kernel(tc, table, w_ref, w_nei, offs, out):
         ident = held.tile([P, P], BF16, name="ident")
         make_identity(nc, ident[:])
 
-        own = psum.tile([P, Q], F32, name="own", tag="feat")
-        nc.tensor.matmul(own[:], ref_w[:], store[:, 0:Q], start=True, stop=True)
+        band = held.tile([P, P + SIDE], BF16, name="band")
+        nc.gpsimd.memset(band[:], 0.0)
+        nc.vector.tensor_copy(
+            band[:].rearrange("p (k w) -> p k w", w=SIDE)[:, :, SIDE - COPIES : SIDE],
+            nei_w[:, 0 : (P + SIDE) // R].rearrange("p (k e) -> p k e", e=COPIES),
+        )
+
+        total = psum.tile([P, Q], F32, name="total", tag="score")
+        nc.tensor.matmul(total[:], ref_w[:], store[:, 0:Q], start=True, stop=False)
+        for r in range(R):
+            first = SIDE - COPIES * (r + 1)
+            nc.tensor.matmul(
+                total[:],
+                band[:, first : first + P],
+                store[:].indirect(offsets[:, r * (Q // 16) : (r + 1) * (Q // 16)]),
+                start=False,
+                stop=(r == R - 1),
+            )
 
         pieces = [offsets[:, b * (BANK // 16) : (b + 1) * (BANK // 16)] for b in range(BANKS)]
-        score = [psum.tile([P, BANK], F32, name=f"score{b}", tag="score") for b in range(BANKS)]
-        for b in range(BANKS):
-            nc.tensor.matmul(score[b][:], nei_w[:], store[:].indirect(pieces[b]), start=True, stop=True)
         feat = [psum.tile([P, BANK], F32, name=f"feat{b}", tag="feat") for b in range(BANKS)]
         for b in range(BANKS):
             nc.tensor.matmul(feat[b][:], ident[:], store[:].indirect(pieces[b]), start=True, stop=True)
 
-        own_flipped = held.tile([P, Q], F32, name="own_flipped", align_bytes=64)
+        total_flipped = held.tile([P, Q], F32, name="total_flipped", align_bytes=64)
         for h in range(Q // P):
-            nc.vector.transpose(own_flipped[:, h * P : (h + 1) * P], own[:, h * P : (h + 1) * P])
-        own_packed = own_flipped[:].rearrange("p (g w) -> p g w", w=SIDE)[:, :, 0]
-        score_flipped = held.tile([P, N], F32, name="score_flipped", align_bytes=64)
-        for b in range(BANKS):
-            nc.vector.transpose(score_flipped[:, b * BANK : (b + 1) * BANK], score[b][:])
-        score_packed = score_flipped[:].rearrange("p (r g w) -> p r g w", g=PACKED_RUN, w=SIDE)[:, :, :, 0]
+            nc.vector.transpose(total_flipped[:, h * P : (h + 1) * P], total[:, h * P : (h + 1) * P])
+        total_packed = total_flipped[:].rearrange("p (g r e) -> p r g e", r=R, e=COPIES)[:, :, :, 0]
 
-        total = held.tile([P, PACKED], F32, name="total")
-        nc.vector.tensor_tensor(
-            total[:].rearrange("p (r g) -> p r g", g=PACKED_RUN),
-            score_packed,
-            own_packed.unsqueeze(1).to_broadcast([P, R, PACKED_RUN]),
-            ALU.add,
-        )
         leaky = held.tile([P, PACKED], F32, name="leaky")
-        nc.vector.scalar_tensor_tensor(leaky[:], total[:], SLOPE, total[:], ALU.mult, ALU.max)
+        nc.vector.scalar_tensor_tensor(
+            leaky[:].rearrange("p (r g) -> p r g", g=PACKED_RUN), total_packed, SLOPE, total_packed, ALU.mult, ALU.max
+        )
         top = held.tile([P, PACKED_RUN], F32, name="top")
         nc.vector.tensor_reduce(top[:], leaky[:].rearrange("p (r g) -> p g r", g=PACKED_RUN), axis=X, op=ALU.max)
         leaky_runs = leaky[:].rearrange("p (r g) -> p r g", g=PACKED_RUN)

@@ -14,14 +14,11 @@ Q = 256
 R = 8
 N = R * Q
 BANK = 512
-RUNS = BANK // Q
 BANKS = N // BANK
+BLOCKS = BANK // P
+HALVES = Q // P
 SLOPE = 0.01
-SIDE = 32
-PACKED = N // SIDE
-PACKED_RUN = Q // SIDE
-PACKED_BANK = BANK // SIDE
-COPIES = SIDE // R
+STEP = 4
 
 FLOPS = 2 * P * P * (N + Q)
 
@@ -30,7 +27,8 @@ def tile_feat_encoder_kernel(tc, table, w_ref, w_nei, offs, out):
     nc = tc.nc
     with (
         tc.tile_pool(name="held", bufs=1) as held,
-        tc.psum_pool(name="psum", bufs=BANKS) as psum,
+        tc.psum_pool(name="narrow", bufs=1) as narrow,
+        tc.psum_pool(name="wide", bufs=6) as wide,
     ):
         store = held.tile([P, NODES], BF16, name="store")
         nc.scalar.dma_start(store[:], table)
@@ -42,18 +40,17 @@ def tile_feat_encoder_kernel(tc, table, w_ref, w_nei, offs, out):
         nc.scalar.dma_start(nei_w[:], w_nei)
         ident = held.tile([P, P], BF16, name="ident")
         make_identity(nc, ident[:])
+        ident32 = held.tile([P, P], F32, name="ident32")
+        make_identity(nc, ident32[:])
 
-        band = held.tile([P, P + SIDE], BF16, name="band")
+        band = held.tile([P, P + STEP * (R - 1)], BF16, name="band")
         nc.gpsimd.memset(band[:], 0.0)
-        nc.vector.tensor_copy(
-            band[:].rearrange("p (k w) -> p k w", w=SIDE)[:, :, SIDE - COPIES : SIDE],
-            nei_w[:, 0 : (P + SIDE) // R].rearrange("p (k e) -> p k e", e=COPIES),
-        )
+        nc.vector.tensor_copy(band[:, STEP * (R - 1) : STEP * (R - 1) + 1], nei_w[:, 0:1])
 
-        total = psum.tile([P, Q], F32, name="total", tag="score")
+        total = narrow.tile([P, Q], F32, name="total", tag="by_node")
         nc.tensor.matmul(total[:], ref_w[:], store[:, 0:Q], start=True, stop=False)
         for r in range(R):
-            first = SIDE - COPIES * (r + 1)
+            first = STEP * (R - 1 - r)
             nc.tensor.matmul(
                 total[:],
                 band[:, first : first + P],
@@ -62,63 +59,70 @@ def tile_feat_encoder_kernel(tc, table, w_ref, w_nei, offs, out):
                 stop=(r == R - 1),
             )
 
-        pieces = [offsets[:, b * (BANK // 16) : (b + 1) * (BANK // 16)] for b in range(BANKS)]
-        feat = [psum.tile([P, BANK], F32, name=f"feat{b}", tag="feat") for b in range(BANKS)]
+        feat = [wide.tile([P, BANK], F32, name=f"feat{b}", tag="wide") for b in range(BANKS)]
         for b in range(BANKS):
-            nc.tensor.matmul(feat[b][:], ident[:], store[:].indirect(pieces[b]), start=True, stop=True)
+            piece = offsets[:, b * (BANK // 16) : (b + 1) * (BANK // 16)]
+            nc.tensor.matmul(feat[b][:], ident[:], store[:].indirect(piece), start=True, stop=True)
 
-        total_flipped = held.tile([P, Q], F32, name="total_flipped", align_bytes=64)
-        for h in range(Q // P):
-            nc.vector.transpose(total_flipped[:, h * P : (h + 1) * P], total[:, h * P : (h + 1) * P])
-        total_packed = total_flipped[:].rearrange("p (g r e) -> p r g e", r=R, e=COPIES)[:, :, :, 0]
+        scaled = held.tile([P, Q], F32, name="scaled")
+        nc.scalar.mul(scaled[:], total[:], -SLOPE)
+        minus = held.tile([P, Q], F32, name="minus")
+        nc.vector.scalar_tensor_tensor(minus[:], total[:], -1.0, scaled[:], ALU.mult, ALU.min)
+        minus_t = narrow.tile([P, Q], F32, name="minus_t", tag="minus_t")
+        for h in range(HALVES):
+            nc.tensor.transpose(minus_t[:, h * P : (h + 1) * P], minus[:, h * P : (h + 1) * P], ident32[:])
+        picked = minus_t[:].rearrange("p (h m e) -> p h m e", h=HALVES, e=STEP)[:, :, 0:R, 0]
 
-        leaky = held.tile([P, PACKED], F32, name="leaky")
-        nc.vector.scalar_tensor_tensor(
-            leaky[:].rearrange("p (r g) -> p r g", g=PACKED_RUN), total_packed, SLOPE, total_packed, ALU.mult, ALU.max
-        )
-        top = held.tile([P, PACKED_RUN], F32, name="top")
-        nc.vector.tensor_reduce(top[:], leaky[:].rearrange("p (r g) -> p g r", g=PACKED_RUN), axis=X, op=ALU.max)
-        leaky_runs = leaky[:].rearrange("p (r g) -> p r g", g=PACKED_RUN)
-        nc.vector.tensor_tensor(
-            leaky_runs, leaky_runs, top[:].unsqueeze(1).to_broadcast([P, R, PACKED_RUN]), ALU.subtract
-        )
-        weight = held.tile([P, PACKED], F32, name="weight")
-        nc.scalar.activation(weight[:], leaky[:], ACT.Exp)
-        den = held.tile([P, PACKED_RUN], F32, name="den")
-        nc.vector.tensor_reduce(den[:], weight[:].rearrange("p (r g) -> p g r", g=PACKED_RUN), axis=X, op=ALU.add)
-        rden = held.tile([P, PACKED_RUN], F32, name="rden")
-        nc.vector.reciprocal(rden[:], den[:])
-
-        num_wide = held.tile([P, BANK], F32, name="num_wide")
-        feat_flipped = [held.tile([P, BANK], F32, name=f"feat_flipped{b}", align_bytes=64) for b in range(BANKS)]
-        prod = [held.tile([P, BANK], F32, name=f"prod{b}") for b in range(BANKS)]
-        for b in range(BANKS):
-            nc.vector.transpose(feat_flipped[b][:], feat[b][:])
-        for b in range(BANKS):
-            nc.vector.tensor_tensor(
-                prod[b][:].rearrange("p (j w) -> p j w", w=SIDE),
-                feat_flipped[b][:].rearrange("p (j w) -> p j w", w=SIDE),
-                weight[:, b * PACKED_BANK : (b + 1) * PACKED_BANK].unsqueeze(2).to_broadcast([P, PACKED_BANK, SIDE]),
-                ALU.mult,
+        shift = held.tile([P, HALVES], F32, name="shift")
+        nc.vector.tensor_reduce(shift[:], picked, axis=X, op=ALU.min)
+        weight = held.tile([P, HALVES * R], F32, name="weight")
+        den = held.tile([P, HALVES], F32, name="den")
+        for h in range(HALVES):
+            nc.scalar.activation(
+                weight[:, h * R : (h + 1) * R],
+                picked[:, h, :],
+                ACT.Exp,
+                bias=shift[:, h : h + 1],
+                scale=-1.0,
+                accum_out=den[:, h : h + 1],
             )
-            if b > 0:
-                nc.vector.tensor_tensor(num_wide[:], prod[0][:] if b == 1 else num_wide[:], prod[b][:], ALU.add)
-        num = held.tile([P, Q], F32, name="num")
-        nc.vector.tensor_tensor(num[:], num_wide[:, 0:Q], num_wide[:, Q:BANK], ALU.add)
-
-        num_blocks = num[:].rearrange("p (g w) -> p g w", w=SIDE)
-        rden_blocks = rden[:].unsqueeze(2).to_broadcast([P, PACKED_RUN, SIDE])
-        neg = held.tile([P, Q], F32, name="neg")
-        nc.vector.scalar_tensor_tensor(
-            neg[:].rearrange("p (g w) -> p g w", w=SIDE), num_blocks, 0.0, rden_blocks, ALU.min, ALU.mult
+        rden = held.tile([P, HALVES], F32, name="rden")
+        nc.vector.reciprocal(rden[:], den[:])
+        share = held.tile([P, HALVES * R], F32, name="share")
+        nc.vector.tensor_tensor(
+            share[:].rearrange("p (h r) -> p h r", r=R),
+            weight[:].rearrange("p (h r) -> p h r", r=R),
+            rden[:].unsqueeze(2).to_broadcast([P, HALVES, R]),
+            ALU.mult,
         )
-        grown = held.tile([P, Q], F32, name="grown")
-        nc.scalar.activation(grown[:], neg[:], ACT.Exp)
-        mean = held.tile([P, Q], F32, name="mean")
-        nc.vector.tensor_tensor(mean[:].rearrange("p (g w) -> p g w", w=SIDE), num_blocks, rden_blocks, ALU.mult)
-        result_flipped = held.tile([P, Q], F32, name="result_flipped", align_bytes=64)
-        nc.vector.scalar_tensor_tensor(result_flipped[:], grown[:], -1.0, mean[:], ALU.add, ALU.max)
 
-        result = held.tile([P, Q], F32, name="result", align_bytes=64)
-        nc.vector.transpose(result[:], result_flipped[:])
+        mean = held.tile([P, Q], F32, name="mean")
+        for b in range(BANKS):
+            feat_sb = held.tile([P, BANK], BF16, name=f"feat_sb{b}")
+            if b % 2 == 0:
+                nc.scalar.copy(feat_sb[:], feat[b][:])
+            else:
+                nc.vector.tensor_copy(feat_sb[:], feat[b][:])
+            feat_t = wide.tile([P, BANK], BF16, name=f"feat_t{b}", tag="wide")
+            for k in range(BLOCKS):
+                nc.tensor.transpose(feat_t[:, k * P : (k + 1) * P], feat_sb[:, k * P : (k + 1) * P], ident[:])
+            for k in range(BLOCKS):
+                r, h = (b * BLOCKS + k) // HALVES, k % HALVES
+                half = mean[:, h * P : (h + 1) * P]
+                turned = feat_t[:, k * P : (k + 1) * P]
+                one = share[:, h * R + r : h * R + r + 1]
+                if r == 0:
+                    nc.vector.tensor_scalar_mul(half, turned, one)
+                else:
+                    nc.vector.scalar_tensor_tensor(half, turned, one, half, ALU.mult, ALU.add)
+
+        mean_t = narrow.tile([P, Q], F32, name="mean_t", tag="by_node")
+        for h in range(HALVES):
+            nc.tensor.transpose(mean_t[:, h * P : (h + 1) * P], mean[:, h * P : (h + 1) * P], ident32[:])
+        grown = held.tile([P, Q], F32, name="grown")
+        nc.scalar.activation(grown[:], mean_t[:], ACT.Exp)
+        rest = held.tile([P, Q], F32, name="rest")
+        nc.vector.tensor_scalar(rest[:], mean_t[:], 0.0, -1.0, ALU.max, ALU.add)
+        result = held.tile([P, Q], F32, name="result")
+        nc.vector.scalar_tensor_tensor(result[:], grown[:], 1.0, rest[:], ALU.min, ALU.add)
         nc.sync.dma_start(out, result[:])

@@ -59,11 +59,6 @@ def tile_feat_encoder_kernel(tc, table, w_ref, w_nei, offs, out):
                 stop=(r == R - 1),
             )
 
-        feat = [wide.tile([P, BANK], F32, name=f"feat{b}", tag="wide") for b in range(BANKS)]
-        for b in range(BANKS):
-            piece = offsets[:, b * (BANK // 16) : (b + 1) * (BANK // 16)]
-            nc.tensor.matmul(feat[b][:], ident[:], store[:].indirect(piece), start=True, stop=True)
-
         scaled = held.tile([P, Q], F32, name="scaled")
         nc.scalar.mul(scaled[:], total[:], -SLOPE)
         minus = held.tile([P, Q], F32, name="minus")
@@ -96,7 +91,15 @@ def tile_feat_encoder_kernel(tc, table, w_ref, w_nei, offs, out):
             ALU.mult,
         )
 
-        mean = held.tile([P, Q], F32, name="mean")
+        feat = [wide.tile([P, BANK], F32, name=f"feat{b}", tag="wide") for b in range(BANKS)]
+        for b in range(BANKS):
+            piece = offsets[:, b * (BANK // 16) : (b + 1) * (BANK // 16)]
+            nc.tensor.matmul(feat[b][:], ident[:], store[:].indirect(piece), start=True, stop=True)
+
+        mean_t = [
+            narrow.tile([P, P], F32, name="mean_t0", tag="by_node"),
+            narrow.tile([P, P], F32, name="mean_t1", tag="minus_t"),
+        ]
         for b in range(BANKS):
             feat_sb = held.tile([P, BANK], BF16, name=f"feat_sb{b}")
             if b % 2 == 0:
@@ -108,21 +111,23 @@ def tile_feat_encoder_kernel(tc, table, w_ref, w_nei, offs, out):
                 nc.tensor.transpose(feat_t[:, k * P : (k + 1) * P], feat_sb[:, k * P : (k + 1) * P], ident[:])
             for k in range(BLOCKS):
                 r, h = (b * BLOCKS + k) // HALVES, k % HALVES
-                half = mean[:, h * P : (h + 1) * P]
                 turned = feat_t[:, k * P : (k + 1) * P]
                 one = share[:, h * R + r : h * R + r + 1]
-                if r == 0:
-                    nc.vector.tensor_scalar_mul(half, turned, one)
+                prod = held.tile([P, P], F32, name=f"prod{r}_{h}")
+                if h == 0:
+                    nc.vector.tensor_scalar_mul(prod[:], turned, one)
                 else:
-                    nc.vector.scalar_tensor_tensor(half, turned, one, half, ALU.mult, ALU.add)
+                    nc.scalar.activation(prod[:], turned, ACT.Copy, scale=one)
+                nc.tensor.matmul(
+                    mean_t[h][:], prod[:], ident32[:], is_transpose=True, start=(r == 0), stop=(r == R - 1)
+                )
 
-        mean_t = narrow.tile([P, Q], F32, name="mean_t", tag="by_node")
-        for h in range(HALVES):
-            nc.tensor.transpose(mean_t[:, h * P : (h + 1) * P], mean[:, h * P : (h + 1) * P], ident32[:])
         grown = held.tile([P, Q], F32, name="grown")
-        nc.scalar.activation(grown[:], mean_t[:], ACT.Exp)
         rest = held.tile([P, Q], F32, name="rest")
-        nc.vector.tensor_scalar(rest[:], mean_t[:], 0.0, -1.0, ALU.max, ALU.add)
         result = held.tile([P, Q], F32, name="result")
-        nc.vector.scalar_tensor_tensor(result[:], grown[:], 1.0, rest[:], ALU.min, ALU.add)
+        for h in range(HALVES):
+            half = slice(h * P, (h + 1) * P)
+            nc.scalar.activation(grown[:, half], mean_t[h][:], ACT.Exp)
+            nc.vector.tensor_scalar(rest[:, half], mean_t[h][:], 0.0, -1.0, ALU.max, ALU.add)
+            nc.vector.scalar_tensor_tensor(result[:, half], grown[:, half], 1.0, rest[:, half], ALU.min, ALU.add)
         nc.sync.dma_start(out, result[:])

@@ -18,7 +18,7 @@ BANKS = N // BANK
 BLOCKS = BANK // P
 HALVES = Q // P
 SLOPE = 0.01
-STEP = 4
+STEP = P // R
 
 FLOPS = 2 * P * P * (N + Q)
 
@@ -36,16 +36,14 @@ def tile_feat_encoder_kernel(tc, table, w_ref, w_nei, offs, out):
         nc.sync.dma_start(ref_w[:], w_ref)
         offsets = held.tile([P, N // 16], U16, name="offsets")
         nc.sync.dma_start(offsets[:], offs)
-        nei_w = held.tile([P, P], BF16, name="nei_w")
-        nc.scalar.dma_start(nei_w[:], w_nei)
+        band = held.tile([P, 2 * P - STEP], BF16, name="band")
+        nc.vector.memset(band[:, 0 : P - STEP], 0.0)
+        nc.vector.memset(band[:, P : 2 * P - STEP], 0.0)
+        nc.scalar.dma_start(band[:, P - STEP : P], w_nei[:, 0:STEP])
         ident = held.tile([P, P], BF16, name="ident")
         make_identity(nc, ident[:])
         ident32 = held.tile([P, P], F32, name="ident32")
         make_identity(nc, ident32[:])
-
-        band = held.tile([P, P + STEP * (R - 1)], BF16, name="band")
-        nc.gpsimd.memset(band[:], 0.0)
-        nc.vector.tensor_copy(band[:, STEP * (R - 1) : STEP * (R - 1) + 1], nei_w[:, 0:1])
 
         total = narrow.tile([P, Q], F32, name="total", tag="by_node")
         nc.tensor.matmul(total[:], ref_w[:], store[:, 0:Q], start=True, stop=False)
@@ -66,7 +64,7 @@ def tile_feat_encoder_kernel(tc, table, w_ref, w_nei, offs, out):
         minus_t = narrow.tile([P, Q], F32, name="minus_t", tag="minus_t")
         for h in range(HALVES):
             nc.tensor.transpose(minus_t[:, h * P : (h + 1) * P], minus[:, h * P : (h + 1) * P], ident32[:])
-        picked = minus_t[:].rearrange("p (h m e) -> p h m e", h=HALVES, e=STEP)[:, :, 0:R, 0]
+        picked = minus_t[:].rearrange("p (h m e) -> p h m e", h=HALVES, e=STEP)[:, :, :, 0]
 
         shift = held.tile([P, HALVES], F32, name="shift")
         nc.vector.tensor_reduce(shift[:], picked, axis=X, op=ALU.min)

@@ -107,17 +107,17 @@ def tile_feat_encoder_kernel(tc, table, w_ref, w_nei, offs, out):
             feat_t = wide.tile([P, BANK], BF16, name=f"feat_t{b}", tag="wide")
             for k in range(BLOCKS):
                 nc.tensor.transpose(feat_t[:, k * P : (k + 1) * P], feat_sb[:, k * P : (k + 1) * P], ident[:])
-            for k in range(BLOCKS):
-                r, h = (b * BLOCKS + k) // HALVES, k % HALVES
-                turned = feat_t[:, k * P : (k + 1) * P]
-                one = share[:, h * R + r : h * R + r + 1]
-                prod = held.tile([P, P], F32, name=f"prod{r}_{h}")
-                if h == 0:
-                    nc.vector.tensor_scalar_mul(prod[:], turned, one)
-                else:
-                    nc.scalar.activation(prod[:], turned, ACT.Copy, scale=one)
+            for h in range(HALVES):
+                even_run = feat_t[:, h * P : (h + 1) * P]
+                odd_run = feat_t[:, (HALVES + h) * P : (HALVES + h + 1) * P]
+                even_share = share[:, h * R + 2 * b : h * R + 2 * b + 1]
+                odd_share = share[:, h * R + 2 * b + 1 : h * R + 2 * b + 2]
+                single = held.tile([P, P], F32, name=f"single{b}_{h}")
+                nc.scalar.activation(single[:], even_run, ACT.Copy, scale=even_share)
+                pair = held.tile([P, P], F32, name=f"pair{b}_{h}")
+                nc.vector.scalar_tensor_tensor(pair[:], odd_run, odd_share, single[:], ALU.mult, ALU.add)
                 nc.tensor.matmul(
-                    mean_t[h][:], prod[:], ident32[:], is_transpose=True, start=(r == 0), stop=(r == R - 1)
+                    mean_t[h][:], pair[:], ident32[:], is_transpose=True, start=(b == 0), stop=(b == BANKS - 1)
                 )
 
         grown = held.tile([P, Q], F32, name="grown")

@@ -104,9 +104,11 @@ def tile_feat_encoder_kernel(tc, table, w_ref, w_nei, offs, out):
                 nc.scalar.copy(feat_sb[:], feat[b][:])
             else:
                 nc.vector.tensor_copy(feat_sb[:], feat[b][:])
-            feat_t = wide.tile([P, BANK], BF16, name=f"feat_t{b}", tag="wide")
+            feat_t = wide.tile([P, BANK], F32, name=f"feat_t{b}", tag="wide")
             for k in range(BLOCKS):
-                nc.tensor.transpose(feat_t[:, k * P : (k + 1) * P], feat_sb[:, k * P : (k + 1) * P], ident[:])
+                nc.tensor.matmul(
+                    feat_t[:, k * P : (k + 1) * P], feat_sb[:, k * P : (k + 1) * P], ident[:], start=True, stop=True
+                )
             for h in range(HALVES):
                 even_run = feat_t[:, h * P : (h + 1) * P]
                 odd_run = feat_t[:, (HALVES + h) * P : (HALVES + h + 1) * P]

@@ -98,29 +98,41 @@ def tile_feat_encoder_kernel(tc, table, w_ref, w_nei, offs, out):
             narrow.tile([P, P], F32, name="mean_t0", tag="by_node"),
             narrow.tile([P, P], F32, name="mean_t1", tag="minus_t"),
         ]
-        for b in range(BANKS):
-            feat_sb = held.tile([P, BANK], BF16, name=f"feat_sb{b}")
-            if b % 2 == 0:
-                nc.scalar.copy(feat_sb[:], feat[b][:])
-            else:
-                nc.vector.tensor_copy(feat_sb[:], feat[b][:])
-            feat_t = wide.tile([P, BANK], F32, name=f"feat_t{b}", tag="wide")
-            for k in range(BLOCKS):
-                nc.tensor.matmul(
-                    feat_t[:, k * P : (k + 1) * P], feat_sb[:, k * P : (k + 1) * P], ident[:], start=True, stop=True
-                )
-            for h in range(HALVES):
-                even_run = feat_t[:, h * P : (h + 1) * P]
-                odd_run = feat_t[:, (HALVES + h) * P : (HALVES + h + 1) * P]
-                even_share = share[:, h * R + 2 * b : h * R + 2 * b + 1]
-                odd_share = share[:, h * R + 2 * b + 1 : h * R + 2 * b + 2]
-                single = held.tile([P, P], F32, name=f"single{b}_{h}")
-                nc.scalar.activation(single[:], even_run, ACT.Copy, scale=even_share)
-                pair = held.tile([P, P], F32, name=f"pair{b}_{h}")
-                nc.vector.scalar_tensor_tensor(pair[:], odd_run, odd_share, single[:], ALU.mult, ALU.add)
-                nc.tensor.matmul(
-                    mean_t[h][:], pair[:], ident32[:], is_transpose=True, start=(b == 0), stop=(b == BANKS - 1)
-                )
+        for first_bank in range(0, BANKS, 2):
+            turned_even = wide.tile([P, BANK], F32, name=f"turned_even{first_bank}", tag="wide")
+            turned_odd = wide.tile([P, BANK], F32, name=f"turned_odd{first_bank}", tag="wide")
+            for b in (first_bank, first_bank + 1):
+                feat_sb = held.tile([P, BANK], BF16, name=f"feat_sb{b}")
+                if b % 2 == 0:
+                    nc.scalar.copy(feat_sb[:], feat[b][:])
+                else:
+                    nc.vector.tensor_copy(feat_sb[:], feat[b][:])
+                for h in range(HALVES):
+                    place = slice(((b % 2) * HALVES + h) * P, ((b % 2) * HALVES + h + 1) * P)
+                    nc.tensor.matmul(
+                        turned_even[:, place], feat_sb[:, h * P : (h + 1) * P], ident[:], start=True, stop=True
+                    )
+                    nc.tensor.matmul(
+                        turned_odd[:, place],
+                        feat_sb[:, (HALVES + h) * P : (HALVES + h + 1) * P],
+                        ident[:],
+                        start=True,
+                        stop=True,
+                    )
+            for b in (first_bank, first_bank + 1):
+                for h in range(HALVES):
+                    place = slice(((b % 2) * HALVES + h) * P, ((b % 2) * HALVES + h + 1) * P)
+                    even_share = share[:, h * R + 2 * b : h * R + 2 * b + 1]
+                    odd_share = share[:, h * R + 2 * b + 1 : h * R + 2 * b + 2]
+                    single = held.tile([P, P], F32, name=f"single{b}_{h}")
+                    nc.scalar.activation(single[:], turned_even[:, place], ACT.Copy, scale=even_share)
+                    pair = held.tile([P, P], F32, name=f"pair{b}_{h}")
+                    nc.vector.scalar_tensor_tensor(
+                        pair[:], turned_odd[:, place], odd_share, single[:], ALU.mult, ALU.add
+                    )
+                    nc.tensor.matmul(
+                        mean_t[h][:], pair[:], ident32[:], is_transpose=True, start=(b == 0), stop=(b == BANKS - 1)
+                    )
 
         grown = held.tile([P, Q], F32, name="grown")
         rest = held.tile([P, Q], F32, name="rest")

@@ -81,13 +81,6 @@ def tile_feat_encoder_kernel(tc, table, w_ref, w_nei, offs, out):
             )
         rden = held.tile([P, HALVES], F32, name="rden")
         nc.vector.reciprocal(rden[:], den[:])
-        share = held.tile([P, HALVES * R], F32, name="share")
-        nc.vector.tensor_tensor(
-            share[:].rearrange("p (h r) -> p h r", r=R),
-            weight[:].rearrange("p (h r) -> p h r", r=R),
-            rden[:].unsqueeze(2).to_broadcast([P, HALVES, R]),
-            ALU.mult,
-        )
 
         feat = [wide.tile([P, BANK], F32, name=f"feat{b}", tag="wide") for b in range(BANKS)]
         for b in range(BANKS):
@@ -122,24 +115,32 @@ def tile_feat_encoder_kernel(tc, table, w_ref, w_nei, offs, out):
             for b in (first_bank, first_bank + 1):
                 for h in range(HALVES):
                     place = slice(((b % 2) * HALVES + h) * P, ((b % 2) * HALVES + h + 1) * P)
-                    even_share = share[:, h * R + 2 * b : h * R + 2 * b + 1]
-                    odd_share = share[:, h * R + 2 * b + 1 : h * R + 2 * b + 2]
+                    even_weight = weight[:, h * R + 2 * b : h * R + 2 * b + 1]
+                    odd_weight = weight[:, h * R + 2 * b + 1 : h * R + 2 * b + 2]
                     single = held.tile([P, P], F32, name=f"single{b}_{h}")
-                    nc.scalar.activation(single[:], turned_even[:, place], ACT.Copy, scale=even_share)
+                    nc.scalar.activation(single[:], turned_even[:, place], ACT.Copy, scale=even_weight)
                     pair = held.tile([P, P], F32, name=f"pair{b}_{h}")
                     nc.vector.scalar_tensor_tensor(
-                        pair[:], turned_odd[:, place], odd_share, single[:], ALU.mult, ALU.add
+                        pair[:], turned_odd[:, place], odd_weight, single[:], ALU.mult, ALU.add
                     )
                     nc.tensor.matmul(
                         mean_t[h][:], pair[:], ident32[:], is_transpose=True, start=(b == 0), stop=(b == BANKS - 1)
                     )
 
+        rden_t = wide.tile([P, Q], F32, name="rden_t", tag="wide")
+        for h in range(HALVES):
+            nc.tensor.transpose(rden_t[:, h * P : (h + 1) * P], rden[:, h : h + 1].to_broadcast([P, P]), ident32[:])
+        rden_rows = held.tile([P, Q], F32, name="rden_rows")
+        nc.vector.tensor_copy(rden_rows[:], rden_t[:])
+
+        mean = held.tile([P, Q], F32, name="mean")
         grown = held.tile([P, Q], F32, name="grown")
         rest = held.tile([P, Q], F32, name="rest")
         result = held.tile([P, Q], F32, name="result")
         for h in range(HALVES):
             half = slice(h * P, (h + 1) * P)
-            nc.scalar.activation(grown[:, half], mean_t[h][:], ACT.Exp)
-            nc.vector.tensor_scalar(rest[:, half], mean_t[h][:], 0.0, -1.0, ALU.max, ALU.add)
+            nc.vector.tensor_tensor(mean[:, half], mean_t[h][:], rden_rows[:, half], ALU.mult)
+            nc.scalar.activation(grown[:, half], mean[:, half], ACT.Exp)
+            nc.vector.tensor_scalar(rest[:, half], mean[:, half], 0.0, -1.0, ALU.max, ALU.add)
             nc.vector.scalar_tensor_tensor(result[:, half], grown[:, half], 1.0, rest[:, half], ALU.min, ALU.add)
         nc.sync.dma_start(out, result[:])

@@ -13,9 +13,6 @@ NODES = 512
 Q = 256
 R = 8
 N = R * Q
-BANK = 512
-BANKS = N // BANK
-BLOCKS = BANK // P
 HALVES = Q // P
 SLOPE = 0.01
 STEP = P // R
@@ -57,14 +54,34 @@ def tile_feat_encoder_kernel(tc, table, w_ref, w_nei, offs, out):
                 stop=(r == R - 1),
             )
 
+
+        def gather_features(r):
+            piece = offsets[:, r * (Q // 16) : (r + 1) * (Q // 16)]
+            nc.tensor.matmul(feat[r][:], ident[:], store[:].indirect(piece), start=True, stop=True)
+
+        def copy_features(r):
+            if r % 2 == 0:
+                nc.scalar.copy(feat_sb[r][:], feat[r][:])
+            else:
+                nc.vector.tensor_copy(feat_sb[r][:], feat[r][:])
+
+        feat = [wide.tile([P, Q], F32, name=f"feat{r}", tag="wide") for r in range(R)]
+        feat_sb = [held.tile([P, Q], BF16, name=f"feat_sb{r}") for r in range(R)]
+
         scaled = held.tile([P, Q], F32, name="scaled")
         nc.scalar.mul(scaled[:], total[:], -SLOPE)
         minus = held.tile([P, Q], F32, name="minus")
         nc.vector.scalar_tensor_tensor(minus[:], total[:], -1.0, scaled[:], ALU.mult, ALU.min)
+        for r in range(R // 2):
+            gather_features(r)
         minus_t = narrow.tile([P, Q], F32, name="minus_t", tag="minus_t")
         for h in range(HALVES):
             nc.tensor.transpose(minus_t[:, h * P : (h + 1) * P], minus[:, h * P : (h + 1) * P], ident32[:])
         picked = minus_t[:].rearrange("p (h m e) -> p h m e", h=HALVES, e=STEP)[:, :, :, 0]
+        for r in range(R // 2, R):
+            gather_features(r)
+        for r in range(R // 2):
+            copy_features(r)
 
         shift = held.tile([P, HALVES], F32, name="shift")
         nc.vector.tensor_reduce(shift[:], picked, axis=X, op=ALU.min)
@@ -79,68 +96,56 @@ def tile_feat_encoder_kernel(tc, table, w_ref, w_nei, offs, out):
                 scale=-1.0,
                 accum_out=den[:, h : h + 1],
             )
+        for r in range(R // 2, R):
+            copy_features(r)
         rden = held.tile([P, HALVES], F32, name="rden")
         nc.vector.reciprocal(rden[:], den[:])
 
-        feat = [wide.tile([P, BANK], F32, name=f"feat{b}", tag="wide") for b in range(BANKS)]
-        for b in range(BANKS):
-            piece = offsets[:, b * (BANK // 16) : (b + 1) * (BANK // 16)]
-            nc.tensor.matmul(feat[b][:], ident[:], store[:].indirect(piece), start=True, stop=True)
+        turned_banks = [wide.tile([P, 2 * Q], BF16, name=f"turned_bank{i}", tag="wide") for i in range(4)]
+        turned = []
+        for r in range(R):
+            bank = turned_banks[2 * (r // (R // 2)) + r % 2]
+            turned.append(bank[:, ((r // 2) % 2) * Q : ((r // 2) % 2 + 1) * Q])
+            for h in range(HALVES):
+                nc.tensor.transpose(turned[r][:, h * P : (h + 1) * P], feat_sb[r][:, h * P : (h + 1) * P], ident[:])
+
+        rden_t = wide.tile([P, Q], F32, name="rden_t", tag="wide")
+        for h in range(HALVES):
+            nc.tensor.transpose(rden_t[:, h * P : (h + 1) * P], rden[:, h : h + 1].to_broadcast([P, P]), ident32[:])
 
         mean_t = [
             narrow.tile([P, P], F32, name="mean_t0", tag="by_node"),
             narrow.tile([P, P], F32, name="mean_t1", tag="minus_t"),
         ]
-        for first_bank in range(0, BANKS, 2):
-            turned_even = wide.tile([P, BANK], F32, name=f"turned_even{first_bank}", tag="wide")
-            turned_odd = wide.tile([P, BANK], F32, name=f"turned_odd{first_bank}", tag="wide")
-            for b in (first_bank, first_bank + 1):
-                feat_sb = held.tile([P, BANK], BF16, name=f"feat_sb{b}")
-                if b % 2 == 0:
-                    nc.scalar.copy(feat_sb[:], feat[b][:])
-                else:
-                    nc.vector.tensor_copy(feat_sb[:], feat[b][:])
-                for h in range(HALVES):
-                    place = slice(((b % 2) * HALVES + h) * P, ((b % 2) * HALVES + h + 1) * P)
-                    nc.tensor.matmul(
-                        turned_even[:, place], feat_sb[:, h * P : (h + 1) * P], ident[:], start=True, stop=True
-                    )
-                    nc.tensor.matmul(
-                        turned_odd[:, place],
-                        feat_sb[:, (HALVES + h) * P : (HALVES + h + 1) * P],
-                        ident[:],
-                        start=True,
-                        stop=True,
-                    )
-            for b in (first_bank, first_bank + 1):
-                for h in range(HALVES):
-                    place = slice(((b % 2) * HALVES + h) * P, ((b % 2) * HALVES + h + 1) * P)
-                    even_weight = weight[:, h * R + 2 * b : h * R + 2 * b + 1]
-                    odd_weight = weight[:, h * R + 2 * b + 1 : h * R + 2 * b + 2]
-                    single = held.tile([P, P], F32, name=f"single{b}_{h}")
-                    nc.scalar.activation(single[:], turned_even[:, place], ACT.Copy, scale=even_weight)
-                    pair = held.tile([P, P], F32, name=f"pair{b}_{h}")
-                    nc.vector.scalar_tensor_tensor(
-                        pair[:], turned_odd[:, place], odd_weight, single[:], ALU.mult, ALU.add
-                    )
-                    nc.tensor.matmul(
-                        mean_t[h][:], pair[:], ident32[:], is_transpose=True, start=(b == 0), stop=(b == BANKS - 1)
-                    )
+        for even in range(0, R, 2):
+            odd = even + 1
+            for h in range(HALVES):
+                half = slice(h * P, (h + 1) * P)
+                single = held.tile([P, P], F32, name=f"single{even}_{h}")
+                nc.scalar.activation(
+                    single[:], turned[even][:, half], ACT.Copy, scale=weight[:, h * R + even : h * R + even + 1]
+                )
+                pair = held.tile([P, P], F32, name=f"pair{even}_{h}")
+                nc.vector.scalar_tensor_tensor(
+                    pair[:], turned[odd][:, half], weight[:, h * R + odd : h * R + odd + 1], single[:], ALU.mult, ALU.add
+                )
+                nc.tensor.matmul(
+                    mean_t[h][:], pair[:], ident32[:], is_transpose=True, start=(even == 0), stop=(odd == R - 1)
+                )
 
-        rden_t = wide.tile([P, Q], F32, name="rden_t", tag="wide")
-        for h in range(HALVES):
-            nc.tensor.transpose(rden_t[:, h * P : (h + 1) * P], rden[:, h : h + 1].to_broadcast([P, P]), ident32[:])
         rden_rows = held.tile([P, Q], F32, name="rden_rows")
-        nc.vector.tensor_copy(rden_rows[:], rden_t[:])
+        nc.scalar.copy(rden_rows[:], rden_t[:])
 
+        halves = [slice(h * P, (h + 1) * P) for h in range(HALVES)]
         mean = held.tile([P, Q], F32, name="mean")
         grown = held.tile([P, Q], F32, name="grown")
         rest = held.tile([P, Q], F32, name="rest")
         result = held.tile([P, Q], F32, name="result")
-        for h in range(HALVES):
-            half = slice(h * P, (h + 1) * P)
+        for h, half in enumerate(halves):
             nc.vector.tensor_tensor(mean[:, half], mean_t[h][:], rden_rows[:, half], ALU.mult)
             nc.scalar.activation(grown[:, half], mean[:, half], ACT.Exp)
+        for half in halves:
             nc.vector.tensor_scalar(rest[:, half], mean[:, half], 0.0, -1.0, ALU.max, ALU.add)
+        for half in halves:
             nc.vector.scalar_tensor_tensor(result[:, half], grown[:, half], 1.0, rest[:, half], ALU.min, ALU.add)
         nc.sync.dma_start(out, result[:])

@@ -72,13 +72,13 @@ def tile_feat_encoder_kernel(tc, table, w_ref, w_nei, offs, out):
         nc.scalar.mul(scaled[:], total[:], -SLOPE)
         minus = held.tile([P, Q], F32, name="minus")
         nc.vector.scalar_tensor_tensor(minus[:], total[:], -1.0, scaled[:], ALU.mult, ALU.min)
-        for r in range(R // 2):
+        for r in range(R - 2):
             gather_features(r)
         minus_t = narrow.tile([P, Q], F32, name="minus_t", tag="minus_t")
         for h in range(HALVES):
             nc.tensor.transpose(minus_t[:, h * P : (h + 1) * P], minus[:, h * P : (h + 1) * P], ident32[:])
         picked = minus_t[:].rearrange("p (h m e) -> p h m e", h=HALVES, e=STEP)[:, :, :, 0]
-        for r in range(R // 2, R):
+        for r in range(R - 2, R):
             gather_features(r)
         for r in range(R // 2):
             copy_features(r)
@@ -148,4 +148,4 @@ def tile_feat_encoder_kernel(tc, table, w_ref, w_nei, offs, out):
             nc.vector.tensor_scalar(rest[:, half], mean[:, half], 0.0, -1.0, ALU.max, ALU.add)
         for half in halves:
             nc.vector.scalar_tensor_tensor(result[:, half], grown[:, half], 1.0, rest[:, half], ALU.min, ALU.add)
-        nc.sync.dma_start(out, result[:])
+            nc.sync.dma_start(out[:, half], result[:, half])

@@ -16,6 +16,7 @@ N = R * Q
 HALVES = Q // P
 SLOPE = 0.01
 STEP = P // R
+AHEAD = 5
 
 FLOPS = 2 * P * P * (N + Q)
 
@@ -72,13 +73,13 @@ def tile_feat_encoder_kernel(tc, table, w_ref, w_nei, offs, out):
         nc.scalar.mul(scaled[:], total[:], -SLOPE)
         minus = held.tile([P, Q], F32, name="minus")
         nc.vector.scalar_tensor_tensor(minus[:], total[:], -1.0, scaled[:], ALU.mult, ALU.min)
-        for r in range(R - 2):
+        for r in range(AHEAD):
             gather_features(r)
         minus_t = narrow.tile([P, Q], F32, name="minus_t", tag="minus_t")
         for h in range(HALVES):
             nc.tensor.transpose(minus_t[:, h * P : (h + 1) * P], minus[:, h * P : (h + 1) * P], ident32[:])
         picked = minus_t[:].rearrange("p (h m e) -> p h m e", h=HALVES, e=STEP)[:, :, :, 0]
-        for r in range(R - 2, R):
+        for r in range(AHEAD, R):
             gather_features(r)
         for r in range(R // 2):
             copy_features(r)

@@ -61,7 +61,7 @@ def tile_feat_encoder_kernel(tc, table, w_ref, w_nei, offs, out):
             nc.tensor.matmul(feat[r][:], ident[:], store[:].indirect(piece), start=True, stop=True)
 
         def copy_features(r):
-            if r % 2 == 0:
+            if r % 2 == 0 and r < R - 2:
                 nc.scalar.copy(feat_sb[r][:], feat[r][:])
             else:
                 nc.vector.tensor_copy(feat_sb[r][:], feat[r][:])

import concourse.mybir as mybir
from concourse.masks import make_identity

BF16 = mybir.dt.bfloat16
F32 = mybir.dt.float32
U16 = mybir.dt.uint16
ALU = mybir.AluOpType
ACT = mybir.ActivationFunctionType
X = mybir.AxisListType.X

P = 128
NODES = 512
Q = 256
R = 8
N = R * Q
HALVES = Q // P
SLOPE = 0.01
STEP = P // R
AHEAD = 5

FLOPS = 2 * P * P * (N + Q)


def tile_feat_encoder_kernel(tc, table, w_ref, w_nei, offs, out):
    nc = tc.nc
    with (
        tc.tile_pool(name="held", bufs=1) as held,
        tc.psum_pool(name="narrow", bufs=1) as narrow,
        tc.psum_pool(name="wide", bufs=6) as wide,
    ):
        store = held.tile([P, NODES], BF16, name="store")
        nc.scalar.dma_start(store[:], table)
        ref_w = held.tile([P, P], BF16, name="ref_w")
        nc.sync.dma_start(ref_w[:], w_ref)
        offsets = held.tile([P, N // 16], U16, name="offsets")
        nc.sync.dma_start(offsets[:], offs)
        band = held.tile([P, 2 * P - STEP], BF16, name="band")
        nc.vector.memset(band[:, 0 : P - STEP], 0.0)
        nc.vector.memset(band[:, P : 2 * P - STEP], 0.0)
        nc.scalar.dma_start(band[:, P - STEP : P], w_nei[:, 0:STEP])
        ident = held.tile([P, P], BF16, name="ident")
        make_identity(nc, ident[:])
        ident32 = held.tile([P, P], F32, name="ident32")
        make_identity(nc, ident32[:])

        total = narrow.tile([P, Q], F32, name="total", tag="by_node")
        nc.tensor.matmul(total[:], ref_w[:], store[:, 0:Q], start=True, stop=False)
        for r in range(R):
            first = STEP * (R - 1 - r)
            nc.tensor.matmul(
                total[:],
                band[:, first : first + P],
                store[:].indirect(offsets[:, r * (Q // 16) : (r + 1) * (Q // 16)]),
                start=False,
                stop=(r == R - 1),
            )


        def gather_features(r):
            piece = offsets[:, r * (Q // 16) : (r + 1) * (Q // 16)]
            nc.tensor.matmul(feat[r][:], ident[:], store[:].indirect(piece), start=True, stop=True)

        def copy_features(r):
            if r % 2 == 0 and r < R - 2:
                nc.scalar.copy(feat_sb[r][:], feat[r][:])
            else:
                nc.vector.tensor_copy(feat_sb[r][:], feat[r][:])

        feat = [wide.tile([P, Q], F32, name=f"feat{r}", tag="wide") for r in range(R)]
        feat_sb = [held.tile([P, Q], BF16, name=f"feat_sb{r}") for r in range(R)]

        scaled = held.tile([P, Q], F32, name="scaled")
        nc.scalar.mul(scaled[:], total[:], -SLOPE)
        minus = held.tile([P, Q], F32, name="minus")
        nc.vector.scalar_tensor_tensor(minus[:], total[:], -1.0, scaled[:], ALU.mult, ALU.min)
        for r in range(AHEAD):
            gather_features(r)
        minus_t = narrow.tile([P, Q], F32, name="minus_t", tag="minus_t")
        for h in range(HALVES):
            nc.tensor.transpose(minus_t[:, h * P : (h + 1) * P], minus[:, h * P : (h + 1) * P], ident32[:])
        picked = minus_t[:].rearrange("p (h m e) -> p h m e", h=HALVES, e=STEP)[:, :, :, 0]
        for r in range(AHEAD, R):
            gather_features(r)
        for r in range(R // 2):
            copy_features(r)

        shift = held.tile([P, HALVES], F32, name="shift")
        nc.vector.tensor_reduce(shift[:], picked, axis=X, op=ALU.min)
        weight = held.tile([P, HALVES * R], F32, name="weight")
        den = held.tile([P, HALVES], F32, name="den")
        for h in range(HALVES):
            nc.scalar.activation(
                weight[:, h * R : (h + 1) * R],
                picked[:, h, :],
                ACT.Exp,
                bias=shift[:, h : h + 1],
                scale=-1.0,
                accum_out=den[:, h : h + 1],
            )
        for r in range(R // 2, R):
            copy_features(r)
        rden = held.tile([P, HALVES], F32, name="rden")
        nc.vector.reciprocal(rden[:], den[:])

        turned_banks = [wide.tile([P, 2 * Q], BF16, name=f"turned_bank{i}", tag="wide") for i in range(4)]
        turned = []
        for r in range(R):
            bank = turned_banks[2 * (r // (R // 2)) + r % 2]
            turned.append(bank[:, ((r // 2) % 2) * Q : ((r // 2) % 2 + 1) * Q])
            for h in range(HALVES):
                nc.tensor.transpose(turned[r][:, h * P : (h + 1) * P], feat_sb[r][:, h * P : (h + 1) * P], ident[:])

        rden_t = wide.tile([P, Q], F32, name="rden_t", tag="wide")
        for h in range(HALVES):
            nc.tensor.transpose(rden_t[:, h * P : (h + 1) * P], rden[:, h : h + 1].to_broadcast([P, P]), ident32[:])

        mean_t = [
            narrow.tile([P, P], F32, name="mean_t0", tag="by_node"),
            narrow.tile([P, P], F32, name="mean_t1", tag="minus_t"),
        ]
        for even in range(0, R, 2):
            odd = even + 1
            for h in range(HALVES):
                half = slice(h * P, (h + 1) * P)
                single = held.tile([P, P], F32, name=f"single{even}_{h}")
                nc.scalar.activation(
                    single[:], turned[even][:, half], ACT.Copy, scale=weight[:, h * R + even : h * R + even + 1]
                )
                pair = held.tile([P, P], F32, name=f"pair{even}_{h}")
                nc.vector.scalar_tensor_tensor(
                    pair[:], turned[odd][:, half], weight[:, h * R + odd : h * R + odd + 1], single[:], ALU.mult, ALU.add
                )
                nc.tensor.matmul(
                    mean_t[h][:], pair[:], ident32[:], is_transpose=True, start=(even == 0), stop=(odd == R - 1)
                )

        rden_rows = held.tile([P, Q], F32, name="rden_rows")
        nc.scalar.copy(rden_rows[:], rden_t[:])

        halves = [slice(h * P, (h + 1) * P) for h in range(HALVES)]
        mean = held.tile([P, Q], F32, name="mean")
        grown = held.tile([P, Q], F32, name="grown")
        rest = held.tile([P, Q], F32, name="rest")
        result = held.tile([P, Q], F32, name="result")
        for h, half in enumerate(halves):
            nc.vector.tensor_tensor(mean[:, half], mean_t[h][:], rden_rows[:, half], ALU.mult)
            nc.scalar.activation(grown[:, half], mean[:, half], ACT.Exp)
        for half in halves:
            nc.vector.tensor_scalar(rest[:, half], mean[:, half], 0.0, -1.0, ALU.max, ALU.add)
        for half in halves:
            nc.vector.scalar_tensor_tensor(result[:, half], grown[:, half], 1.0, rest[:, half], ALU.min, ALU.add)
            nc.sync.dma_start(out[:, half], result[:, half])
